import numpy as np
import ml_dtypes


def mxq(x, axis, fmt="e4m3"):
    dtype, down = {"e4m3": (ml_dtypes.float8_e4m3fn, 7), "e5m2": (ml_dtypes.float8_e5m2, 14)}[fmt]
    v = np.moveaxis(np.asarray(x, np.float32).astype(ml_dtypes.bfloat16).astype(np.float64), axis, -1)
    blocks = v.reshape(v.shape[:-1] + (-1, 32))
    amax = np.abs(blocks).max(-1, keepdims=True)
    byte = np.maximum(np.where(amax > 0, np.frexp(amax)[1] - 1 + 127, 0) - down, 1)
    scale = np.exp2(byte - 127.0)
    codes = (blocks / scale).astype(np.float32).astype(dtype).astype(np.float64)
    return np.moveaxis((codes * scale).reshape(v.shape), -1, axis)


WIDE = False


def mx_kscale(k):
    if not WIDE:
        return np.ones(k)
    levels = np.array([10, -10, 5, -5, 0])
    a = np.random.permutation(np.resize(levels, k // 512 * 4)).reshape(k // 512, 4)
    idx = np.arange(k)
    return np.exp2(a[idx // 512, idx % 128 // 32])


BF16 = ml_dtypes.bfloat16


def bf(x):
    return np.asarray(x, np.float32).astype(BF16)


def f64(x):
    return np.asarray(x).astype(np.float64)


B, S, I0, I1, I2, I3, I4, O0, O1, O2, O3, O4, R1, R2, R3, R4 = 4, 2048, 4, 4, 2, 2, 16, 2, 2, 2, 2, 8, 16, 512, 1024, 512
IL, OL = I0 * I1 * I2 * I3, O0 * O1 * O2 * O3
IN, OUT = IL * I4, OL * O4


def setup_inputs():
    s = mx_kscale(R4)
    a = mx_kscale(IN)[::I4]
    return {"x": bf(np.random.standard_normal((B, S, IN)) / np.repeat(a, I4)),
            "t3": bf(np.random.standard_normal((IL, OL, R4)) * s * a[:, None, None]),
            "core4": bf(np.random.standard_normal((R4, I4, O4, 1)) / np.sqrt(R4 * IN) / s[:, None, None, None]),
            "bias": bf(np.random.standard_normal(OUT))}


def reference(x, t3, core4, bias):
    p = mxq(f64(t3).reshape(IL * OL, R4), 1, "e4m3") @ mxq(f64(core4).reshape(R4, I4 * O4), 0, "e4m3")
    m = p.reshape(IL, OL, I4, O4, 1).transpose(0, 2, 1, 3, 4).reshape(IN, OUT, 1)[:, :, 0]
    y = (mxq(f64(x).reshape(B * S, IN), 1, "e4m3") @ mxq(m, 0, "e4m3")) + f64(bias)
    return y.reshape(B, S, OUT)

@@ -1,0 +1,228 @@
+from contextlib import ExitStack
+
+import concourse.mybir as mybir
+from concourse.masks import make_identity
+
+F32 = mybir.dt.float32
+BF16 = mybir.dt.bfloat16
+U32 = mybir.dt.uint32
+U8 = mybir.dt.uint8
+I32 = mybir.dt.int32
+FP8X4 = mybir.dt.float8_e4m3fn_x4
+ADD = mybir.AluOpType.add
+
+P = 128
+N_CHUNKS = 16
+X_BUFS = 10
+FLOPS = 2 * 1024 * 512 * 128 + 2 * 8192 * 1024 * 128
+STORE_AFTER = {3: 0, 7: 4, 11: 8, 13: 12, 14: 14, 15: 15}
+
+
+def tile_linear2mpo_pb_t_kernel(tc, x, t3, core4, bias, out):
+    nc = tc.nc
+    with ExitStack() as ctx:
+        const = ctx.enter_context(tc.tile_pool(name="const", bufs=1))
+        xpool = ctx.enter_context(tc.tile_pool(name="xpool", bufs=X_BUFS))
+        gpool = ctx.enter_context(tc.tile_pool(name="gpool", bufs=3))
+        cpool = ctx.enter_context(tc.tile_pool(name="cpool", bufs=6))
+        ps_t = ctx.enter_context(tc.psum_pool(name="ps_t", bufs=6))
+        ps_y = ctx.enter_context(tc.psum_pool(name="ps_y", bufs=2))
+
+        x_v = x.rearrange("b (q t) k -> (b q) (t k)", t=64)
+        out_v = out.rearrange("b (q t) n -> (b q) (t n)", t=64)
+        t3_v = t3.rearrange("(a jh jl) o r -> jh (jl o) a r", a=4, jh=2, jl=8)
+        c4_v = core4.rearrange("(u q e) i o z -> q u (e i o z)", u=2, q=128, e=2)
+        bias_v = bias.rearrange("(o n) -> o n", o=1)
+
+        idf = const.tile([P, P], F32, name="idf")
+        make_identity(nc, idf[:])
+        idb = const.tile([P, P], BF16, name="idb")
+        make_identity(nc, idb[:])
+        ones = const.tile([P, P], BF16, name="ones")
+        nc.vector.memset(ones[:], 1.0)
+        bias_row = const.tile([P, 512], BF16, name="bias_row")
+        nc.vector.memset(bias_row[:], 0.0)
+        t3_codes = const.tile([P, 1088], U32, name="t3_codes", align_bytes=64)
+        t3_scales = const.tile([P, 1088], U8, name="t3_scales", align_bytes=64)
+        nc.vector.memset(t3_codes[:, 1024:1088].bitcast(I32), 0)
+        nc.vector.memset(t3_scales[:, 1024:1088].bitcast(I32), 0)
+
+        c4raw = const.tile([P, 512], BF16, name="c4raw")
+        nc.sync.dma_start(out=c4raw[:].rearrange("p (u f) -> p u f", u=2), in_=c4_v)
+        t3_sb = const.tile([P, 4096], BF16, name="t3_sb")
+        for jh in range(2):
+            nc.sync.dma_start(
+                out=t3_sb[:, 2048 * jh : 2048 * (jh + 1)].rearrange("p (a r) -> p a r", a=4),
+                in_=t3_v[jh],
+            )
+        for k in range(4):
+            nc.scalar.dma_start(out=bias_row[0:1, 128 * k : 128 * (k + 1)], in_=bias_v)
+
+        x_tiles = {}
+
+        def load_x(c):
+            x_sb = xpool.tile([P, 4096], BF16, name="x_sb", tag="x_sb")
+            nc.sync.dma_start(out=x_sb[:], in_=x_v[:, 4096 * c : 4096 * (c + 1)])
+            x_tiles[c] = x_sb
+
+        for c in range(X_BUFS):
+            load_x(c)
+
+        yb = ps_y.tile([P, 512], F32, name="yb", tag="y")
+        nc.tensor.matmul(out=yb[:], lhsT=ones[:], rhs=bias_row[:], start=True, stop=True)
+        bias_bc = const.tile([P, 512], F32, name="bias_bc")
+        nc.scalar.copy(out=bias_bc[:], in_=yb[:])
+
+        gc4 = const.tile([P, 512], BF16, name="gc4", align_bytes=64)
+        for e in range(2):
+            nc.vector.tensor_copy(
+                out=gc4[:].rearrange("p (o e h t) -> p e o h t", o=8, e=2, h=8, t=4)[:, e],
+                in_=c4raw[:].rearrange("p (t h e o) -> p e o h t", t=4, h=8, e=2, o=8)[:, e],
+            )
+        c4_codes = const.tile([P, 128], U32, name="c4_codes", align_bytes=64)
+        c4_scales = const.tile([P, 128], U8, name="c4_scales", align_bytes=64)
+        nc.vector.quantize_mx(out=c4_codes[:].bitcast(FP8X4), scales=c4_scales[:], in_=gc4[:])
+
+        t3w = t3_sb[:].bitcast(F32)
+        gt3 = const.tile([P, 4096], BF16, name="gt3", align_bytes=64)
+        gt3w = gt3[:].bitcast(F32)
+        for jh in range(2):
+            for g in range(2):
+                tp = ps_t.tile([P, 512], F32, name="tp", tag="xt")
+                for u in range(2):
+                    for u1 in range(2):
+                        v = 2 * u + u1
+                        w0 = 1024 * jh + 256 * (2 * g + u) + 128 * u1
+                        nc.tensor.transpose(
+                            out=tp[:, 128 * v : 128 * (v + 1)], in_=t3w[:, w0 : w0 + 128], identity=idf[:]
+                        )
+                dst = gt3w[:, 1024 * jh : 1024 * (jh + 1)].rearrange(
+                    "p (jl g o v) -> p g jl o v", jl=8, g=2, o=16, v=4
+                )[:, g]
+                src = tp[:].rearrange("p (v jl o) -> p jl o v", v=4, jl=8, o=16)
+                if g == 0:
+                    nc.vector.tensor_copy(out=dst, in_=src)
+                else:
+                    nc.scalar.copy(out=dst, in_=src)
+        for jh in range(2):
+            nc.vector.quantize_mx(
+                out=t3_codes[:, 512 * jh : 512 * (jh + 1)].bitcast(FP8X4),
+                scales=t3_scales[:, 512 * jh : 512 * (jh + 1)],
+                in_=gt3[:, 2048 * jh : 2048 * (jh + 1)],
+            )
+
+        pm = const.tile([P, 2048], BF16, name="pm")
+        for b in range(4):
+            if b < 2:
+                sp = ps_y.tile([P, 512], F32, name="sp", tag="y")
+            else:
+                sp = ps_t.tile([P, 512], F32, name="sp2", tag="xt")
+            for jq in range(4):
+                j = 4 * b + jq
+                nc.tensor.matmul_mx(
+                    out=sp[:, 128 * jq : 128 * (jq + 1)],
+                    lhsT=t3_codes[:, 64 * j : 64 * j + 128].bitcast(FP8X4),
+                    lhsT_scale=t3_scales[:, 64 * j : 64 * j + 128],
+                    rhs=c4_codes[:].bitcast(FP8X4),
+                    rhs_scale=c4_scales[:],
+                    start=True,
+                    stop=True,
+                )
+            dst = pm[:].rearrange("p (tr b jq h) -> p b tr jq h", tr=16, b=4, jq=4, h=8)[:, b]
+            src = sp[:].rearrange("p (jq tr h) -> p tr jq h", jq=4, tr=16, h=8)
+            if b % 2 == 0:
+                nc.vector.tensor_copy(out=dst, in_=src)
+            else:
+                nc.scalar.copy(out=dst, in_=src)
+
+        grouped = {}
+        codes = {}
+        y_tiles = {}
+        out_sb = const.tile([P, 8192], F32, name="out_sb")
+
+        def transpose_chunk(c):
+            xw = x_tiles[c][:].bitcast(F32)
+            g_sb = gpool.tile([P, 4096], BF16, name="g_sb", tag="g_sb", align_bytes=64)
+            gw = g_sb[:].bitcast(F32)
+            for t in range(4):
+                bank = ps_t.tile([P, 512], F32, name="xt", tag="xt")
+                for a in range(4):
+                    w0 = 512 * t + 128 * a
+                    nc.tensor.transpose(
+                        out=bank[:, 128 * a : 128 * (a + 1)], in_=xw[:, w0 : w0 + 128], identity=idf[:]
+                    )
+                nc.scalar.copy(
+                    out=gw[:, 512 * t : 512 * (t + 1)].rearrange("p (g r u) -> p g r u", g=2, r=128, u=2),
+                    in_=bank[:].rearrange("p (g u r) -> p g r u", g=2, u=2, r=128),
+                )
+            grouped[c] = g_sb
+
+        def quantise_chunk(c):
+            x_codes = cpool.tile([P, 1024], U32, name="x_codes", tag="x_codes", align_bytes=64)
+            x_scales = cpool.tile([P, 1024], U8, name="x_scales", tag="x_scales", align_bytes=64)
+            nc.vector.quantize_mx(out=x_codes[:].bitcast(FP8X4), scales=x_scales[:], in_=grouped[c][:])
+            codes[c] = (x_codes, x_scales)
+
+        def multiply_chunk(c):
+            x_codes, x_scales = codes[c]
+            y = ps_y.tile([P, 512], F32, name="y", tag="y")
+            for t in range(4):
+                for g in range(2):
+                    s0 = 128 * (2 * t + g)
+                    nc.tensor.matmul_mx(
+                        out=y[:, 128 * t : 128 * (t + 1)],
+                        lhsT=x_codes[:, s0 : s0 + 128].bitcast(FP8X4),
+                        lhsT_scale=x_scales[:, s0 : s0 + 128],
+                        rhs=m_codes[:, 128 * g : 128 * (g + 1)].bitcast(FP8X4),
+                        rhs_scale=m_scales[:, 128 * g : 128 * (g + 1)],
+                        start=(g == 0),
+                        stop=(g == 1),
+                    )
+            y_tiles[c] = y
+
+        def finish_chunk(c):
+            nc.vector.tensor_tensor(
+                out=out_sb[:, 512 * c : 512 * (c + 1)], in0=y_tiles[c][:], in1=bias_bc[:], op=ADD
+            )
+            if c in STORE_AFTER:
+                lo = 512 * STORE_AFTER[c]
+                hi = 512 * (c + 1)
+                nc.sync.dma_start(out=out_v[:, lo:hi], in_=out_sb[:, lo:hi])
+
+        transpose_chunk(0)
+        load_x(X_BUFS)
+
+        gm = const.tile([P, 1024], BF16, name="gm", align_bytes=64)
+        for ob in range(2):
+            mp = ps_t.tile([P, 1024], BF16, name="mp", tag="xt")
+            for trl in range(8):
+                tr = 8 * ob + trl
+                nc.tensor.transpose(
+                    out=mp[:, 128 * trl : 128 * (trl + 1)], in_=pm[:, 128 * tr : 128 * (tr + 1)], identity=idb[:]
+                )
+            for e in range(2):
+                dst = gm[:].rearrange("p (q ob ol u e) -> p ob e q ol u", q=32, ob=2, ol=4, u=2, e=2)[:, ob, e]
+                src = mp[:].rearrange("p (ol e d q u) -> p e d q ol u", ol=4, e=2, d=2, q=32, u=2)[:, e, 0]
+                if ob == 0:
+                    nc.vector.tensor_copy(out=dst, in_=src)
+                else:
+                    nc.scalar.copy(out=dst, in_=src)
+        m_codes = const.tile([P, 256], U32, name="m_codes", align_bytes=64)
+        m_scales = const.tile([P, 256], U8, name="m_scales", align_bytes=64)
+        nc.vector.quantize_mx(out=m_codes[:].bitcast(FP8X4), scales=m_scales[:], in_=gm[:])
+
+        transpose_chunk(1)
+        load_x(X_BUFS + 1)
+        quantise_chunk(0)
+
+        for i in range(2, N_CHUNKS + 3):
+            if i < N_CHUNKS:
+                transpose_chunk(i)
+                if i + X_BUFS < N_CHUNKS:
+                    load_x(i + X_BUFS)
+            if 0 <= i - 3 < N_CHUNKS:
+                finish_chunk(i - 3)
+            if i - 1 < N_CHUNKS:
+                quantise_chunk(i - 1)
+            if i - 2 < N_CHUNKS:
+                multiply_chunk(i - 2)

@@ -27,6 +27,7 @@ def tile_linear2mpo_pb_t_kernel(tc, x, t3, core4, bias, out):
         cpool = ctx.enter_context(tc.tile_pool(name="cpool", bufs=6))
         ps_t = ctx.enter_context(tc.psum_pool(name="ps_t", bufs=6))
         ps_y = ctx.enter_context(tc.psum_pool(name="ps_y", bufs=2))
+        ctx.enter_context(tc.manual_schedule())
 
         x_v = x.rearrange("b (q t) k -> (b q) (t k)", t=64)
         out_v = out.rearrange("b (q t) n -> (b q) (t n)", t=64)

@@ -15,6 +15,7 @@ P = 128
 N_CHUNKS = 16
 X_BUFS = 10
 FLOPS = 2 * 1024 * 512 * 128 + 2 * 8192 * 1024 * 128
+VECTOR_COPIES = (2, 4, 6, 8, 10, 12, 14)
 STORE_AFTER = {3: 0, 7: 4, 11: 8, 13: 12, 14: 14, 15: 15}
 
 
@@ -69,11 +70,6 @@ def tile_linear2mpo_pb_t_kernel(tc, x, t3, core4, bias, out):
         for c in range(X_BUFS):
             load_x(c)
 
-        yb = ps_y.tile([P, 512], F32, name="yb", tag="y")
-        nc.tensor.matmul(out=yb[:], lhsT=ones[:], rhs=bias_row[:], start=True, stop=True)
-        bias_bc = const.tile([P, 512], F32, name="bias_bc")
-        nc.scalar.copy(out=bias_bc[:], in_=yb[:])
-
         gc4 = const.tile([P, 512], BF16, name="gc4", align_bytes=64)
         for e in range(2):
             nc.vector.tensor_copy(
@@ -112,6 +108,11 @@ def tile_linear2mpo_pb_t_kernel(tc, x, t3, core4, bias, out):
                 in_=gt3[:, 2048 * jh : 2048 * (jh + 1)],
             )
 
+        yb = ps_y.tile([P, 512], F32, name="yb", tag="y")
+        nc.tensor.matmul(out=yb[:], lhsT=ones[:], rhs=bias_row[:], start=True, stop=True)
+        bias_bc = const.tile([P, 512], F32, name="bias_bc")
+        nc.scalar.copy(out=bias_bc[:], in_=yb[:])
+
         pm = const.tile([P, 2048], BF16, name="pm")
         for b in range(4):
             if b < 2:
@@ -131,14 +132,12 @@ def tile_linear2mpo_pb_t_kernel(tc, x, t3, core4, bias, out):
                 )
             dst = pm[:].rearrange("p (tr b jq h) -> p b tr jq h", tr=16, b=4, jq=4, h=8)[:, b]
             src = sp[:].rearrange("p (jq tr h) -> p tr jq h", jq=4, tr=16, h=8)
-            if b % 2 == 0:
-                nc.vector.tensor_copy(out=dst, in_=src)
-            else:
-                nc.scalar.copy(out=dst, in_=src)
+            nc.vector.tensor_copy(out=dst, in_=src)
 
         grouped = {}
         codes = {}
         y_tiles = {}
+        left_for_vector = {}
         out_sb = const.tile([P, 8192], F32, name="out_sb")
 
         def transpose_chunk(c):
@@ -152,11 +151,18 @@ def tile_linear2mpo_pb_t_kernel(tc, x, t3, core4, bias, out):
                     nc.tensor.transpose(
                         out=bank[:, 128 * a : 128 * (a + 1)], in_=xw[:, w0 : w0 + 128], identity=idf[:]
                     )
-                nc.scalar.copy(
-                    out=gw[:, 512 * t : 512 * (t + 1)].rearrange("p (g r u) -> p g r u", g=2, r=128, u=2),
-                    in_=bank[:].rearrange("p (g u r) -> p g r u", g=2, u=2, r=128),
-                )
+                dst = gw[:, 512 * t : 512 * (t + 1)].rearrange("p (g r u) -> p g r u", g=2, r=128, u=2)
+                src = bank[:].rearrange("p (g u r) -> p g r u", g=2, u=2, r=128)
+                if t == 3 and c in VECTOR_COPIES:
+                    left_for_vector[c] = (dst, src)
+                else:
+                    nc.scalar.copy(out=dst, in_=src)
             grouped[c] = g_sb
+
+        def vector_copy(c):
+            if c in left_for_vector:
+                dst, src = left_for_vector[c]
+                nc.vector.tensor_copy(out=dst, in_=src)
 
         def quantise_chunk(c):
             x_codes = cpool.tile([P, 1024], U32, name="x_codes", tag="x_codes", align_bytes=64)
@@ -204,10 +210,7 @@ def tile_linear2mpo_pb_t_kernel(tc, x, t3, core4, bias, out):
             for e in range(2):
                 dst = gm[:].rearrange("p (q ob ol u e) -> p ob e q ol u", q=32, ob=2, ol=4, u=2, e=2)[:, ob, e]
                 src = mp[:].rearrange("p (ol e d q u) -> p e d q ol u", ol=4, e=2, d=2, q=32, u=2)[:, e, 0]
-                if ob == 0:
-                    nc.vector.tensor_copy(out=dst, in_=src)
-                else:
-                    nc.scalar.copy(out=dst, in_=src)
+                nc.vector.tensor_copy(out=dst, in_=src)
         m_codes = const.tile([P, 256], U32, name="m_codes", align_bytes=64)
         m_scales = const.tile([P, 256], U8, name="m_scales", align_bytes=64)
         nc.vector.quantize_mx(out=m_codes[:].bitcast(FP8X4), scales=m_scales[:], in_=gm[:])
@@ -225,5 +228,6 @@ def tile_linear2mpo_pb_t_kernel(tc, x, t3, core4, bias, out):
                 finish_chunk(i - 3)
             if i - 1 < N_CHUNKS:
                 quantise_chunk(i - 1)
+            vector_copy(i)
             if i - 2 < N_CHUNKS:
                 multiply_chunk(i - 2)

@@ -12,11 +12,13 @@ FP8X4 = mybir.dt.float8_e4m3fn_x4
 ADD = mybir.AluOpType.add
 
 P = 128
-N_CHUNKS = 16
-X_BUFS = 10
 FLOPS = 2 * 1024 * 512 * 128 + 2 * 8192 * 1024 * 128
+UNITS = tuple((4 * c, 4) for c in range(15)) + ((60, 2), (62, 2))
+N_UNITS = len(UNITS)
+LAST_FULL = 14
+X_BUFS = 10
 VECTOR_COPIES = (2, 4, 6, 8, 10, 12, 14)
-STORE_AFTER = {3: 0, 7: 4, 11: 8, 13: 12, 14: 14, 15: 15}
+STORE_AFTER = {3: 0, 7: 4, 11: 8, 13: 12, 14: 14, 16: 15}
 
 
 def tile_linear2mpo_pb_t_kernel(tc, x, t3, core4, bias, out):
@@ -40,35 +42,39 @@ def tile_linear2mpo_pb_t_kernel(tc, x, t3, core4, bias, out):
         make_identity(nc, idf[:])
         idb = const.tile([P, P], BF16, name="idb")
         make_identity(nc, idb[:])
-        ones = const.tile([P, P], BF16, name="ones")
-        nc.vector.memset(ones[:], 1.0)
         bias_row = const.tile([P, 512], BF16, name="bias_row")
         nc.vector.memset(bias_row[:], 0.0)
+        ones = const.tile([P, P], BF16, name="ones")
+        nc.vector.memset(ones[:], 1.0)
         t3_codes = const.tile([P, 1088], U32, name="t3_codes", align_bytes=64)
         t3_scales = const.tile([P, 1088], U8, name="t3_scales", align_bytes=64)
         nc.vector.memset(t3_codes[:, 1024:1088].bitcast(I32), 0)
         nc.vector.memset(t3_scales[:, 1024:1088].bitcast(I32), 0)
 
         c4raw = const.tile([P, 512], BF16, name="c4raw")
-        nc.sync.dma_start(out=c4raw[:].rearrange("p (u f) -> p u f", u=2), in_=c4_v)
         t3_sb = const.tile([P, 4096], BF16, name="t3_sb")
         for jh in range(2):
-            nc.sync.dma_start(
-                out=t3_sb[:, 2048 * jh : 2048 * (jh + 1)].rearrange("p (a r) -> p a r", a=4),
-                in_=t3_v[jh],
-            )
-        for k in range(4):
-            nc.scalar.dma_start(out=bias_row[0:1, 128 * k : 128 * (k + 1)], in_=bias_v)
+            for g in range(2):
+                e0 = 2048 * jh + 1024 * g
+                nc.sync.dma_start(
+                    out=t3_sb[:, e0 : e0 + 1024].rearrange("p (a r) -> p a r", a=2),
+                    in_=t3_v[jh][:, 2 * g : 2 * g + 2, :],
+                )
+                if jh == 0 and g == 0:
+                    nc.sync.dma_start(out=c4raw[:].rearrange("p (u f) -> p u f", u=2), in_=c4_v)
+        nc.scalar.dma_start(out=bias_row[0:1, 0:128], in_=bias_v)
 
         x_tiles = {}
 
-        def load_x(c):
-            x_sb = xpool.tile([P, 4096], BF16, name="x_sb", tag="x_sb")
-            nc.sync.dma_start(out=x_sb[:], in_=x_v[:, 4096 * c : 4096 * (c + 1)])
-            x_tiles[c] = x_sb
+        def load_x(u):
+            if u < N_UNITS:
+                t0, nt = UNITS[u]
+                x_sb = xpool.tile([P, 4096], BF16, name="x_sb", tag="x_sb")
+                nc.sync.dma_start(out=x_sb[:, 0 : 1024 * nt], in_=x_v[:, 1024 * t0 : 1024 * (t0 + nt)])
+                x_tiles[u] = x_sb
 
-        for c in range(X_BUFS):
-            load_x(c)
+        for u in range(X_BUFS):
+            load_x(u)
 
         gc4 = const.tile([P, 512], BF16, name="gc4", align_bytes=64)
         for e in range(2):
@@ -111,7 +117,8 @@ def tile_linear2mpo_pb_t_kernel(tc, x, t3, core4, bias, out):
         yb = ps_y.tile([P, 512], F32, name="yb", tag="y")
         nc.tensor.matmul(out=yb[:], lhsT=ones[:], rhs=bias_row[:], start=True, stop=True)
         bias_bc = const.tile([P, 512], F32, name="bias_bc")
-        nc.scalar.copy(out=bias_bc[:], in_=yb[:])
+        for k in range(4):
+            nc.scalar.copy(out=bias_bc[:, 128 * k : 128 * (k + 1)], in_=yb[:, 0:128])
 
         pm = const.tile([P, 2048], BF16, name="pm")
         for b in range(4):
@@ -130,9 +137,10 @@ def tile_linear2mpo_pb_t_kernel(tc, x, t3, core4, bias, out):
                     start=True,
                     stop=True,
                 )
-            dst = pm[:].rearrange("p (tr b jq h) -> p b tr jq h", tr=16, b=4, jq=4, h=8)[:, b]
-            src = sp[:].rearrange("p (jq tr h) -> p tr jq h", jq=4, tr=16, h=8)
-            nc.vector.tensor_copy(out=dst, in_=src)
+            nc.vector.tensor_copy(
+                out=pm[:].rearrange("p (tr b jq h) -> p b tr jq h", tr=16, b=4, jq=4, h=8)[:, b],
+                in_=sp[:].rearrange("p (jq tr h) -> p tr jq h", jq=4, tr=16, h=8),
+            )
 
         grouped = {}
         codes = {}
@@ -140,11 +148,12 @@ def tile_linear2mpo_pb_t_kernel(tc, x, t3, core4, bias, out):
         left_for_vector = {}
         out_sb = const.tile([P, 8192], F32, name="out_sb")
 
-        def transpose_chunk(c):
-            xw = x_tiles[c][:].bitcast(F32)
+        def transpose_unit(u):
+            nt = UNITS[u][1]
+            xw = x_tiles[u][:].bitcast(F32)
             g_sb = gpool.tile([P, 4096], BF16, name="g_sb", tag="g_sb", align_bytes=64)
             gw = g_sb[:].bitcast(F32)
-            for t in range(4):
+            for t in range(nt):
                 bank = ps_t.tile([P, 512], F32, name="xt", tag="xt")
                 for a in range(4):
                     w0 = 512 * t + 128 * a
@@ -153,27 +162,34 @@ def tile_linear2mpo_pb_t_kernel(tc, x, t3, core4, bias, out):
                     )
                 dst = gw[:, 512 * t : 512 * (t + 1)].rearrange("p (g r u) -> p g r u", g=2, r=128, u=2)
                 src = bank[:].rearrange("p (g u r) -> p g r u", g=2, u=2, r=128)
-                if t == 3 and c in VECTOR_COPIES:
-                    left_for_vector[c] = (dst, src)
+                if t == nt - 1 and u in VECTOR_COPIES:
+                    left_for_vector[u] = (dst, src)
                 else:
                     nc.scalar.copy(out=dst, in_=src)
-            grouped[c] = g_sb
+            grouped[u] = g_sb
+            load_x(u + X_BUFS)
 
-        def vector_copy(c):
-            if c in left_for_vector:
-                dst, src = left_for_vector[c]
+        def vector_copy(u):
+            if u in left_for_vector:
+                dst, src = left_for_vector[u]
                 nc.vector.tensor_copy(out=dst, in_=src)
 
-        def quantise_chunk(c):
+        def quantise_unit(u):
+            nt = UNITS[u][1]
             x_codes = cpool.tile([P, 1024], U32, name="x_codes", tag="x_codes", align_bytes=64)
             x_scales = cpool.tile([P, 1024], U8, name="x_scales", tag="x_scales", align_bytes=64)
-            nc.vector.quantize_mx(out=x_codes[:].bitcast(FP8X4), scales=x_scales[:], in_=grouped[c][:])
-            codes[c] = (x_codes, x_scales)
+            nc.vector.quantize_mx(
+                out=x_codes[:, 0 : 256 * nt].bitcast(FP8X4),
+                scales=x_scales[:, 0 : 256 * nt],
+                in_=grouped[u][:, 0 : 1024 * nt],
+            )
+            codes[u] = (x_codes, x_scales)
 
-        def multiply_chunk(c):
-            x_codes, x_scales = codes[c]
+        def multiply_unit(u):
+            nt = UNITS[u][1]
+            x_codes, x_scales = codes[u]
             y = ps_y.tile([P, 512], F32, name="y", tag="y")
-            for t in range(4):
+            for t in range(nt):
                 for g in range(2):
                     s0 = 128 * (2 * t + g)
                     nc.tensor.matmul_mx(
@@ -185,19 +201,22 @@ def tile_linear2mpo_pb_t_kernel(tc, x, t3, core4, bias, out):
                         start=(g == 0),
                         stop=(g == 1),
                     )
-            y_tiles[c] = y
+            y_tiles[u] = y
 
-        def finish_chunk(c):
+        def finish_unit(u):
+            t0, nt = UNITS[u]
             nc.vector.tensor_tensor(
-                out=out_sb[:, 512 * c : 512 * (c + 1)], in0=y_tiles[c][:], in1=bias_bc[:], op=ADD
+                out=out_sb[:, 128 * t0 : 128 * (t0 + nt)],
+                in0=y_tiles[u][:, 0 : 128 * nt],
+                in1=bias_bc[:, 0 : 128 * nt],
+                op=ADD,
             )
-            if c in STORE_AFTER:
-                lo = 512 * STORE_AFTER[c]
-                hi = 512 * (c + 1)
+            if u in STORE_AFTER:
+                lo = 128 * UNITS[STORE_AFTER[u]][0]
+                hi = 128 * (t0 + nt)
                 nc.sync.dma_start(out=out_v[:, lo:hi], in_=out_sb[:, lo:hi])
 
-        transpose_chunk(0)
-        load_x(X_BUFS)
+        transpose_unit(0)
 
         gm = const.tile([P, 1024], BF16, name="gm", align_bytes=64)
         for ob in range(2):
@@ -208,26 +227,36 @@ def tile_linear2mpo_pb_t_kernel(tc, x, t3, core4, bias, out):
                     out=mp[:, 128 * trl : 128 * (trl + 1)], in_=pm[:, 128 * tr : 128 * (tr + 1)], identity=idb[:]
                 )
             for e in range(2):
-                dst = gm[:].rearrange("p (q ob ol u e) -> p ob e q ol u", q=32, ob=2, ol=4, u=2, e=2)[:, ob, e]
-                src = mp[:].rearrange("p (ol e d q u) -> p e d q ol u", ol=4, e=2, d=2, q=32, u=2)[:, e, 0]
-                nc.vector.tensor_copy(out=dst, in_=src)
+                nc.vector.tensor_copy(
+                    out=gm[:].rearrange("p (q ob ol u e) -> p ob e q ol u", q=32, ob=2, ol=4, u=2, e=2)[:, ob, e],
+                    in_=mp[:].rearrange("p (ol e d q u) -> p e d q ol u", ol=4, e=2, d=2, q=32, u=2)[:, e, 0],
+                )
         m_codes = const.tile([P, 256], U32, name="m_codes", align_bytes=64)
         m_scales = const.tile([P, 256], U8, name="m_scales", align_bytes=64)
         nc.vector.quantize_mx(out=m_codes[:].bitcast(FP8X4), scales=m_scales[:], in_=gm[:])
 
-        transpose_chunk(1)
-        load_x(X_BUFS + 1)
-        quantise_chunk(0)
+        transpose_unit(1)
+        quantise_unit(0)
 
-        for i in range(2, N_CHUNKS + 3):
-            if i < N_CHUNKS:
-                transpose_chunk(i)
-                if i + X_BUFS < N_CHUNKS:
-                    load_x(i + X_BUFS)
-            if 0 <= i - 3 < N_CHUNKS:
-                finish_chunk(i - 3)
-            if i - 1 < N_CHUNKS:
-                quantise_chunk(i - 1)
+        for i in range(2, LAST_FULL + 1):
+            transpose_unit(i)
+            if i >= 3:
+                finish_unit(i - 3)
+            quantise_unit(i - 1)
             vector_copy(i)
-            if i - 2 < N_CHUNKS:
-                multiply_chunk(i - 2)
+            multiply_unit(i - 2)
+
+        transpose_unit(15)
+        transpose_unit(16)
+        finish_unit(12)
+        quantise_unit(14)
+        multiply_unit(13)
+        multiply_unit(14)
+        quantise_unit(15)
+        finish_unit(13)
+        quantise_unit(16)
+        multiply_unit(15)
+        multiply_unit(16)
+        finish_unit(14)
+        finish_unit(15)
+        finish_unit(16)

@@ -26,7 +26,7 @@ def tile_linear2mpo_pb_t_kernel(tc, x, t3, core4, bias, out):
     with ExitStack() as ctx:
         const = ctx.enter_context(tc.tile_pool(name="const", bufs=1))
         xpool = ctx.enter_context(tc.tile_pool(name="xpool", bufs=X_BUFS))
-        gpool = ctx.enter_context(tc.tile_pool(name="gpool", bufs=3))
+        gpool = ctx.enter_context(tc.tile_pool(name="gpool", bufs=4))
         cpool = ctx.enter_context(tc.tile_pool(name="cpool", bufs=6))
         ps_t = ctx.enter_context(tc.psum_pool(name="ps_t", bufs=6))
         ps_y = ctx.enter_context(tc.psum_pool(name="ps_y", bufs=2))
@@ -238,13 +238,24 @@ def tile_linear2mpo_pb_t_kernel(tc, x, t3, core4, bias, out):
         transpose_unit(1)
         quantise_unit(0)
 
-        for i in range(2, LAST_FULL + 1):
-            transpose_unit(i)
-            if i >= 3:
-                finish_unit(i - 3)
-            quantise_unit(i - 1)
-            vector_copy(i)
-            multiply_unit(i - 2)
+        for a in range(2, LAST_FULL, 2):
+            transpose_unit(a)
+            transpose_unit(a + 1)
+            quantise_unit(a - 1)
+            if a >= 4:
+                finish_unit(a - 4)
+            vector_copy(a)
+            if a >= 4:
+                finish_unit(a - 3)
+            quantise_unit(a)
+            multiply_unit(a - 2)
+            multiply_unit(a - 1)
+        transpose_unit(14)
+        quantise_unit(13)
+        finish_unit(10)
+        vector_copy(14)
+        finish_unit(11)
+        multiply_unit(12)
 
         transpose_unit(15)
         transpose_unit(16)

@@ -13,12 +13,13 @@ ADD = mybir.AluOpType.add
 
 P = 128
 FLOPS = 2 * 1024 * 512 * 128 + 2 * 8192 * 1024 * 128
+
 UNITS = tuple((4 * c, 4) for c in range(15)) + ((60, 2), (62, 2))
 N_UNITS = len(UNITS)
 LAST_FULL = 14
 X_BUFS = 10
 VECTOR_COPIES = (2, 4, 6, 8, 10, 12, 14)
-STORE_AFTER = {3: 0, 7: 4, 11: 8, 13: 12, 14: 14, 16: 15}
+STORE_AFTER = {3: 0, 7: 4, 11: 8, 12: 12, 13: 13, 14: 14, 16: 15}
 
 
 def tile_linear2mpo_pb_t_kernel(tc, x, t3, core4, bias, out):
@@ -26,7 +27,7 @@ def tile_linear2mpo_pb_t_kernel(tc, x, t3, core4, bias, out):
     with ExitStack() as ctx:
         const = ctx.enter_context(tc.tile_pool(name="const", bufs=1))
         xpool = ctx.enter_context(tc.tile_pool(name="xpool", bufs=X_BUFS))
-        gpool = ctx.enter_context(tc.tile_pool(name="gpool", bufs=4))
+        gpool = ctx.enter_context(tc.tile_pool(name="gpool", bufs=3))
         cpool = ctx.enter_context(tc.tile_pool(name="cpool", bufs=6))
         ps_t = ctx.enter_context(tc.psum_pool(name="ps_t", bufs=6))
         ps_y = ctx.enter_context(tc.psum_pool(name="ps_y", bufs=2))
@@ -34,8 +35,8 @@ def tile_linear2mpo_pb_t_kernel(tc, x, t3, core4, bias, out):
 
         x_v = x.rearrange("b (q t) k -> (b q) (t k)", t=64)
         out_v = out.rearrange("b (q t) n -> (b q) (t n)", t=64)
-        t3_v = t3.rearrange("(a jh jl) o r -> jh (jl o) a r", a=4, jh=2, jl=8)
-        c4_v = core4.rearrange("(u q e) i o z -> q u (e i o z)", u=2, q=128, e=2)
+        t3_v = t3.rearrange("(a j) (oh ol) r -> (j oh) a (ol r)", a=4, j=16, oh=8, ol=2)
+        c4_v = core4.rearrange("(s q d) i o z -> q s (d i o z)", s=2, q=128, d=2)
         bias_v = bias.rearrange("(o n) -> o n", o=1)
 
         idf = const.tile([P, P], F32, name="idf")
@@ -53,34 +54,32 @@ def tile_linear2mpo_pb_t_kernel(tc, x, t3, core4, bias, out):
 
         c4raw = const.tile([P, 512], BF16, name="c4raw")
         t3_sb = const.tile([P, 4096], BF16, name="t3_sb")
-        for jh in range(2):
-            for g in range(2):
-                e0 = 2048 * jh + 1024 * g
-                nc.sync.dma_start(
-                    out=t3_sb[:, e0 : e0 + 1024].rearrange("p (a r) -> p a r", a=2),
-                    in_=t3_v[jh][:, 2 * g : 2 * g + 2, :],
-                )
-                if jh == 0 and g == 0:
-                    nc.sync.dma_start(out=c4raw[:].rearrange("p (u f) -> p u f", u=2), in_=c4_v)
+        for g in range(2):
+            nc.sync.dma_start(
+                out=t3_sb[:, 2048 * g : 2048 * (g + 1)].rearrange("p (a f) -> p a f", a=2),
+                in_=t3_v[:, 2 * g : 2 * g + 2, :],
+            )
+            if g == 0:
+                nc.sync.dma_start(out=c4raw[:].rearrange("p (s f) -> p s f", s=2), in_=c4_v)
         nc.scalar.dma_start(out=bias_row[0:1, 0:128], in_=bias_v)
 
         x_tiles = {}
 
-        def load_x(u):
-            if u < N_UNITS:
-                t0, nt = UNITS[u]
+        def load_x(n):
+            if n < N_UNITS:
+                t0, nt = UNITS[n]
                 x_sb = xpool.tile([P, 4096], BF16, name="x_sb", tag="x_sb")
                 nc.sync.dma_start(out=x_sb[:, 0 : 1024 * nt], in_=x_v[:, 1024 * t0 : 1024 * (t0 + nt)])
-                x_tiles[u] = x_sb
+                x_tiles[n] = x_sb
 
-        for u in range(X_BUFS):
-            load_x(u)
+        for n in range(X_BUFS):
+            load_x(n)
 
         gc4 = const.tile([P, 512], BF16, name="gc4", align_bytes=64)
         for e in range(2):
             nc.vector.tensor_copy(
-                out=gc4[:].rearrange("p (o e h t) -> p e o h t", o=8, e=2, h=8, t=4)[:, e],
-                in_=c4raw[:].rearrange("p (t h e o) -> p e o h t", t=4, h=8, e=2, o=8)[:, e],
+                out=gc4[:].rearrange("p (o e h v) -> p e o h v", o=8, e=2, h=8, v=4)[:, e],
+                in_=c4raw[:].rearrange("p (v h e o) -> p e o h v", v=4, h=8, e=2, o=8)[:, e],
             )
         c4_codes = const.tile([P, 128], U32, name="c4_codes", align_bytes=64)
         c4_scales = const.tile([P, 128], U8, name="c4_scales", align_bytes=64)
@@ -89,20 +88,18 @@ def tile_linear2mpo_pb_t_kernel(tc, x, t3, core4, bias, out):
         t3w = t3_sb[:].bitcast(F32)
         gt3 = const.tile([P, 4096], BF16, name="gt3", align_bytes=64)
         gt3w = gt3[:].bitcast(F32)
-        for jh in range(2):
-            for g in range(2):
+        for g in range(2):
+            for ol in range(2):
                 tp = ps_t.tile([P, 512], F32, name="tp", tag="xt")
                 for u in range(2):
-                    for u1 in range(2):
-                        v = 2 * u + u1
-                        w0 = 1024 * jh + 256 * (2 * g + u) + 128 * u1
+                    for s in range(2):
+                        us = 2 * u + s
+                        w0 = 512 * (2 * g + u) + 256 * ol + 128 * s
                         nc.tensor.transpose(
-                            out=tp[:, 128 * v : 128 * (v + 1)], in_=t3w[:, w0 : w0 + 128], identity=idf[:]
+                            out=tp[:, 128 * us : 128 * (us + 1)], in_=t3w[:, w0 : w0 + 128], identity=idf[:]
                         )
-                dst = gt3w[:, 1024 * jh : 1024 * (jh + 1)].rearrange(
-                    "p (jl g o v) -> p g jl o v", jl=8, g=2, o=16, v=4
-                )[:, g]
-                src = tp[:].rearrange("p (v jl o) -> p jl o v", v=4, jl=8, o=16)
+                dst = gt3w.rearrange("p (j g oh ol us) -> p g ol j oh us", j=16, g=2, oh=8, ol=2, us=4)[:, g, ol]
+                src = tp[:].rearrange("p (us j oh) -> p j oh us", us=4, j=16, oh=8)
                 if g == 0:
                     nc.vector.tensor_copy(out=dst, in_=src)
                 else:
@@ -138,8 +135,8 @@ def tile_linear2mpo_pb_t_kernel(tc, x, t3, core4, bias, out):
                     stop=True,
                 )
             nc.vector.tensor_copy(
-                out=pm[:].rearrange("p (tr b jq h) -> p b tr jq h", tr=16, b=4, jq=4, h=8)[:, b],
-                in_=sp[:].rearrange("p (jq tr h) -> p tr jq h", jq=4, tr=16, h=8),
+                out=pm[:].rearrange("p (oe b jq h) -> p b oe jq h", oe=16, b=4, jq=4, h=8)[:, b],
+                in_=sp[:].rearrange("p (jq oe h) -> p oe jq h", jq=4, oe=16, h=8),
             )
 
         grouped = {}
@@ -148,46 +145,46 @@ def tile_linear2mpo_pb_t_kernel(tc, x, t3, core4, bias, out):
         left_for_vector = {}
         out_sb = const.tile([P, 8192], F32, name="out_sb")
 
-        def transpose_unit(u):
-            nt = UNITS[u][1]
-            xw = x_tiles[u][:].bitcast(F32)
+        def transpose_unit(n):
+            nt = UNITS[n][1]
+            xw = x_tiles[n][:].bitcast(F32)
             g_sb = gpool.tile([P, 4096], BF16, name="g_sb", tag="g_sb", align_bytes=64)
             gw = g_sb[:].bitcast(F32)
             for t in range(nt):
                 bank = ps_t.tile([P, 512], F32, name="xt", tag="xt")
-                for a in range(4):
-                    w0 = 512 * t + 128 * a
+                for gu in range(4):
+                    w0 = 512 * t + 128 * gu
                     nc.tensor.transpose(
-                        out=bank[:, 128 * a : 128 * (a + 1)], in_=xw[:, w0 : w0 + 128], identity=idf[:]
+                        out=bank[:, 128 * gu : 128 * (gu + 1)], in_=xw[:, w0 : w0 + 128], identity=idf[:]
                     )
                 dst = gw[:, 512 * t : 512 * (t + 1)].rearrange("p (g r u) -> p g r u", g=2, r=128, u=2)
                 src = bank[:].rearrange("p (g u r) -> p g r u", g=2, u=2, r=128)
-                if t == nt - 1 and u in VECTOR_COPIES:
-                    left_for_vector[u] = (dst, src)
+                if t == nt - 1 and n in VECTOR_COPIES:
+                    left_for_vector[n] = (dst, src)
                 else:
                     nc.scalar.copy(out=dst, in_=src)
-            grouped[u] = g_sb
-            load_x(u + X_BUFS)
+            grouped[n] = g_sb
+            load_x(n + X_BUFS)
 
-        def vector_copy(u):
-            if u in left_for_vector:
-                dst, src = left_for_vector[u]
+        def vector_copy(n):
+            if n in left_for_vector:
+                dst, src = left_for_vector[n]
                 nc.vector.tensor_copy(out=dst, in_=src)
 
-        def quantise_unit(u):
-            nt = UNITS[u][1]
+        def quantise_unit(n):
+            nt = UNITS[n][1]
             x_codes = cpool.tile([P, 1024], U32, name="x_codes", tag="x_codes", align_bytes=64)
             x_scales = cpool.tile([P, 1024], U8, name="x_scales", tag="x_scales", align_bytes=64)
             nc.vector.quantize_mx(
                 out=x_codes[:, 0 : 256 * nt].bitcast(FP8X4),
                 scales=x_scales[:, 0 : 256 * nt],
-                in_=grouped[u][:, 0 : 1024 * nt],
+                in_=grouped[n][:, 0 : 1024 * nt],
             )
-            codes[u] = (x_codes, x_scales)
+            codes[n] = (x_codes, x_scales)
 
-        def multiply_unit(u):
-            nt = UNITS[u][1]
-            x_codes, x_scales = codes[u]
+        def multiply_unit(n):
+            nt = UNITS[n][1]
+            x_codes, x_scales = codes[n]
             y = ps_y.tile([P, 512], F32, name="y", tag="y")
             for t in range(nt):
                 for g in range(2):
@@ -201,18 +198,18 @@ def tile_linear2mpo_pb_t_kernel(tc, x, t3, core4, bias, out):
                         start=(g == 0),
                         stop=(g == 1),
                     )
-            y_tiles[u] = y
+            y_tiles[n] = y
 
-        def finish_unit(u):
-            t0, nt = UNITS[u]
+        def finish_unit(n):
+            t0, nt = UNITS[n]
             nc.vector.tensor_tensor(
                 out=out_sb[:, 128 * t0 : 128 * (t0 + nt)],
-                in0=y_tiles[u][:, 0 : 128 * nt],
+                in0=y_tiles[n][:, 0 : 128 * nt],
                 in1=bias_bc[:, 0 : 128 * nt],
                 op=ADD,
             )
-            if u in STORE_AFTER:
-                lo = 128 * UNITS[STORE_AFTER[u]][0]
+            if n in STORE_AFTER:
+                lo = 128 * UNITS[STORE_AFTER[n]][0]
                 hi = 128 * (t0 + nt)
                 nc.sync.dma_start(out=out_v[:, lo:hi], in_=out_sb[:, lo:hi])
 
@@ -221,15 +218,17 @@ def tile_linear2mpo_pb_t_kernel(tc, x, t3, core4, bias, out):
         gm = const.tile([P, 1024], BF16, name="gm", align_bytes=64)
         for ob in range(2):
             mp = ps_t.tile([P, 1024], BF16, name="mp", tag="xt")
-            for trl in range(8):
-                tr = 8 * ob + trl
+            for oel in range(8):
+                oe = 8 * ob + oel
                 nc.tensor.transpose(
-                    out=mp[:, 128 * trl : 128 * (trl + 1)], in_=pm[:, 128 * tr : 128 * (tr + 1)], identity=idb[:]
+                    out=mp[:, 128 * oel : 128 * (oel + 1)], in_=pm[:, 128 * oe : 128 * (oe + 1)], identity=idb[:]
                 )
             for e in range(2):
                 nc.vector.tensor_copy(
-                    out=gm[:].rearrange("p (q ob ol u e) -> p ob e q ol u", q=32, ob=2, ol=4, u=2, e=2)[:, ob, e],
-                    in_=mp[:].rearrange("p (ol e d q u) -> p e d q ol u", ol=4, e=2, d=2, q=32, u=2)[:, e, 0],
+                    out=gm[:].rearrange("p (go ob ol u e) -> p ob e go ol u", go=32, ob=2, ol=4, u=2, e=2)[:, ob, e],
+                    in_=mp[:].rearrange("p (ol e half go u) -> p e half go ol u", ol=4, e=2, half=2, go=32, u=2)[
+                        :, e, 0
+                    ],
                 )
         m_codes = const.tile([P, 256], U32, name="m_codes", align_bytes=64)
         m_scales = const.tile([P, 256], U8, name="m_scales", align_bytes=64)
@@ -238,24 +237,13 @@ def tile_linear2mpo_pb_t_kernel(tc, x, t3, core4, bias, out):
         transpose_unit(1)
         quantise_unit(0)
 
-        for a in range(2, LAST_FULL, 2):
-            transpose_unit(a)
-            transpose_unit(a + 1)
-            quantise_unit(a - 1)
-            if a >= 4:
-                finish_unit(a - 4)
-            vector_copy(a)
-            if a >= 4:
-                finish_unit(a - 3)
-            quantise_unit(a)
-            multiply_unit(a - 2)
-            multiply_unit(a - 1)
-        transpose_unit(14)
-        quantise_unit(13)
-        finish_unit(10)
-        vector_copy(14)
-        finish_unit(11)
-        multiply_unit(12)
+        for i in range(2, LAST_FULL + 1):
+            transpose_unit(i)
+            if i >= 3:
+                finish_unit(i - 3)
+            quantise_unit(i - 1)
+            vector_copy(i)
+            multiply_unit(i - 2)
 
         transpose_unit(15)
         transpose_unit(16)

from contextlib import ExitStack

import concourse.mybir as mybir
from concourse.masks import make_identity

F32 = mybir.dt.float32
BF16 = mybir.dt.bfloat16
U32 = mybir.dt.uint32
U8 = mybir.dt.uint8
I32 = mybir.dt.int32
FP8X4 = mybir.dt.float8_e4m3fn_x4
ADD = mybir.AluOpType.add

P = 128
FLOPS = 2 * 1024 * 512 * 128 + 2 * 8192 * 1024 * 128

UNITS = tuple((4 * c, 4) for c in range(15)) + ((60, 2), (62, 2))
N_UNITS = len(UNITS)
LAST_FULL = 14
X_BUFS = 10
VECTOR_COPIES = (2, 4, 6, 8, 10, 12, 14)
STORE_AFTER = {3: 0, 7: 4, 11: 8, 12: 12, 13: 13, 14: 14, 16: 15}


def tile_linear2mpo_pb_t_kernel(tc, x, t3, core4, bias, out):
    nc = tc.nc
    with ExitStack() as ctx:
        const = ctx.enter_context(tc.tile_pool(name="const", bufs=1))
        xpool = ctx.enter_context(tc.tile_pool(name="xpool", bufs=X_BUFS))
        gpool = ctx.enter_context(tc.tile_pool(name="gpool", bufs=3))
        cpool = ctx.enter_context(tc.tile_pool(name="cpool", bufs=6))
        ps_t = ctx.enter_context(tc.psum_pool(name="ps_t", bufs=6))
        ps_y = ctx.enter_context(tc.psum_pool(name="ps_y", bufs=2))
        ctx.enter_context(tc.manual_schedule())

        x_v = x.rearrange("b (q t) k -> (b q) (t k)", t=64)
        out_v = out.rearrange("b (q t) n -> (b q) (t n)", t=64)
        t3_v = t3.rearrange("(a j) (oh ol) r -> (j oh) a (ol r)", a=4, j=16, oh=8, ol=2)
        c4_v = core4.rearrange("(s q d) i o z -> q s (d i o z)", s=2, q=128, d=2)
        bias_v = bias.rearrange("(o n) -> o n", o=1)

        idf = const.tile([P, P], F32, name="idf")
        make_identity(nc, idf[:])
        idb = const.tile([P, P], BF16, name="idb")
        make_identity(nc, idb[:])
        bias_row = const.tile([P, 512], BF16, name="bias_row")
        nc.vector.memset(bias_row[:], 0.0)
        ones = const.tile([P, P], BF16, name="ones")
        nc.vector.memset(ones[:], 1.0)
        t3_codes = const.tile([P, 1088], U32, name="t3_codes", align_bytes=64)
        t3_scales = const.tile([P, 1088], U8, name="t3_scales", align_bytes=64)
        nc.vector.memset(t3_codes[:, 1024:1088].bitcast(I32), 0)
        nc.vector.memset(t3_scales[:, 1024:1088].bitcast(I32), 0)

        c4raw = const.tile([P, 512], BF16, name="c4raw")
        t3_sb = const.tile([P, 4096], BF16, name="t3_sb")
        for g in range(2):
            nc.sync.dma_start(
                out=t3_sb[:, 2048 * g : 2048 * (g + 1)].rearrange("p (a f) -> p a f", a=2),
                in_=t3_v[:, 2 * g : 2 * g + 2, :],
            )
            if g == 0:
                nc.sync.dma_start(out=c4raw[:].rearrange("p (s f) -> p s f", s=2), in_=c4_v)
        nc.scalar.dma_start(out=bias_row[0:1, 0:128], in_=bias_v)

        x_tiles = {}

        def load_x(n):
            if n < N_UNITS:
                t0, nt = UNITS[n]
                x_sb = xpool.tile([P, 4096], BF16, name="x_sb", tag="x_sb")
                nc.sync.dma_start(out=x_sb[:, 0 : 1024 * nt], in_=x_v[:, 1024 * t0 : 1024 * (t0 + nt)])
                x_tiles[n] = x_sb

        for n in range(X_BUFS):
            load_x(n)

        gc4 = const.tile([P, 512], BF16, name="gc4", align_bytes=64)
        for e in range(2):
            nc.vector.tensor_copy(
                out=gc4[:].rearrange("p (o e h v) -> p e o h v", o=8, e=2, h=8, v=4)[:, e],
                in_=c4raw[:].rearrange("p (v h e o) -> p e o h v", v=4, h=8, e=2, o=8)[:, e],
            )
        c4_codes = const.tile([P, 128], U32, name="c4_codes", align_bytes=64)
        c4_scales = const.tile([P, 128], U8, name="c4_scales", align_bytes=64)
        nc.vector.quantize_mx(out=c4_codes[:].bitcast(FP8X4), scales=c4_scales[:], in_=gc4[:])

        t3w = t3_sb[:].bitcast(F32)
        gt3 = const.tile([P, 4096], BF16, name="gt3", align_bytes=64)
        gt3w = gt3[:].bitcast(F32)
        for g in range(2):
            for ol in range(2):
                tp = ps_t.tile([P, 512], F32, name="tp", tag="xt")
                for u in range(2):
                    for s in range(2):
                        us = 2 * u + s
                        w0 = 512 * (2 * g + u) + 256 * ol + 128 * s
                        nc.tensor.transpose(
                            out=tp[:, 128 * us : 128 * (us + 1)], in_=t3w[:, w0 : w0 + 128], identity=idf[:]
                        )
                dst = gt3w.rearrange("p (j g oh ol us) -> p g ol j oh us", j=16, g=2, oh=8, ol=2, us=4)[:, g, ol]
                src = tp[:].rearrange("p (us j oh) -> p j oh us", us=4, j=16, oh=8)
                if g == 0:
                    nc.vector.tensor_copy(out=dst, in_=src)
                else:
                    nc.scalar.copy(out=dst, in_=src)
        for jh in range(2):
            nc.vector.quantize_mx(
                out=t3_codes[:, 512 * jh : 512 * (jh + 1)].bitcast(FP8X4),
                scales=t3_scales[:, 512 * jh : 512 * (jh + 1)],
                in_=gt3[:, 2048 * jh : 2048 * (jh + 1)],
            )

        yb = ps_y.tile([P, 512], F32, name="yb", tag="y")
        nc.tensor.matmul(out=yb[:], lhsT=ones[:], rhs=bias_row[:], start=True, stop=True)
        bias_bc = const.tile([P, 512], F32, name="bias_bc")
        for k in range(4):
            nc.scalar.copy(out=bias_bc[:, 128 * k : 128 * (k + 1)], in_=yb[:, 0:128])

        pm = const.tile([P, 2048], BF16, name="pm")
        for b in range(4):
            if b < 2:
                sp = ps_y.tile([P, 512], F32, name="sp", tag="y")
            else:
                sp = ps_t.tile([P, 512], F32, name="sp2", tag="xt")
            for jq in range(4):
                j = 4 * b + jq
                nc.tensor.matmul_mx(
                    out=sp[:, 128 * jq : 128 * (jq + 1)],
                    lhsT=t3_codes[:, 64 * j : 64 * j + 128].bitcast(FP8X4),
                    lhsT_scale=t3_scales[:, 64 * j : 64 * j + 128],
                    rhs=c4_codes[:].bitcast(FP8X4),
                    rhs_scale=c4_scales[:],
                    start=True,
                    stop=True,
                )
            nc.vector.tensor_copy(
                out=pm[:].rearrange("p (oe b jq h) -> p b oe jq h", oe=16, b=4, jq=4, h=8)[:, b],
                in_=sp[:].rearrange("p (jq oe h) -> p oe jq h", jq=4, oe=16, h=8),
            )

        grouped = {}
        codes = {}
        y_tiles = {}
        left_for_vector = {}
        out_sb = const.tile([P, 8192], F32, name="out_sb")

        def transpose_unit(n):
            nt = UNITS[n][1]
            xw = x_tiles[n][:].bitcast(F32)
            g_sb = gpool.tile([P, 4096], BF16, name="g_sb", tag="g_sb", align_bytes=64)
            gw = g_sb[:].bitcast(F32)
            for t in range(nt):
                bank = ps_t.tile([P, 512], F32, name="xt", tag="xt")
                for gu in range(4):
                    w0 = 512 * t + 128 * gu
                    nc.tensor.transpose(
                        out=bank[:, 128 * gu : 128 * (gu + 1)], in_=xw[:, w0 : w0 + 128], identity=idf[:]
                    )
                dst = gw[:, 512 * t : 512 * (t + 1)].rearrange("p (g r u) -> p g r u", g=2, r=128, u=2)
                src = bank[:].rearrange("p (g u r) -> p g r u", g=2, u=2, r=128)
                if t == nt - 1 and n in VECTOR_COPIES:
                    left_for_vector[n] = (dst, src)
                else:
                    nc.scalar.copy(out=dst, in_=src)
            grouped[n] = g_sb
            load_x(n + X_BUFS)

        def vector_copy(n):
            if n in left_for_vector:
                dst, src = left_for_vector[n]
                nc.vector.tensor_copy(out=dst, in_=src)

        def quantise_unit(n):
            nt = UNITS[n][1]
            x_codes = cpool.tile([P, 1024], U32, name="x_codes", tag="x_codes", align_bytes=64)
            x_scales = cpool.tile([P, 1024], U8, name="x_scales", tag="x_scales", align_bytes=64)
            nc.vector.quantize_mx(
                out=x_codes[:, 0 : 256 * nt].bitcast(FP8X4),
                scales=x_scales[:, 0 : 256 * nt],
                in_=grouped[n][:, 0 : 1024 * nt],
            )
            codes[n] = (x_codes, x_scales)

        def multiply_unit(n):
            nt = UNITS[n][1]
            x_codes, x_scales = codes[n]
            y = ps_y.tile([P, 512], F32, name="y", tag="y")
            for t in range(nt):
                for g in range(2):
                    s0 = 128 * (2 * t + g)
                    nc.tensor.matmul_mx(
                        out=y[:, 128 * t : 128 * (t + 1)],
                        lhsT=x_codes[:, s0 : s0 + 128].bitcast(FP8X4),
                        lhsT_scale=x_scales[:, s0 : s0 + 128],
                        rhs=m_codes[:, 128 * g : 128 * (g + 1)].bitcast(FP8X4),
                        rhs_scale=m_scales[:, 128 * g : 128 * (g + 1)],
                        start=(g == 0),
                        stop=(g == 1),
                    )
            y_tiles[n] = y

        def finish_unit(n):
            t0, nt = UNITS[n]
            nc.vector.tensor_tensor(
                out=out_sb[:, 128 * t0 : 128 * (t0 + nt)],
                in0=y_tiles[n][:, 0 : 128 * nt],
                in1=bias_bc[:, 0 : 128 * nt],
                op=ADD,
            )
            if n in STORE_AFTER:
                lo = 128 * UNITS[STORE_AFTER[n]][0]
                hi = 128 * (t0 + nt)
                nc.sync.dma_start(out=out_v[:, lo:hi], in_=out_sb[:, lo:hi])

        transpose_unit(0)

        gm = const.tile([P, 1024], BF16, name="gm", align_bytes=64)
        for ob in range(2):
            mp = ps_t.tile([P, 1024], BF16, name="mp", tag="xt")
            for oel in range(8):
                oe = 8 * ob + oel
                nc.tensor.transpose(
                    out=mp[:, 128 * oel : 128 * (oel + 1)], in_=pm[:, 128 * oe : 128 * (oe + 1)], identity=idb[:]
                )
            for e in range(2):
                nc.vector.tensor_copy(
                    out=gm[:].rearrange("p (go ob ol u e) -> p ob e go ol u", go=32, ob=2, ol=4, u=2, e=2)[:, ob, e],
                    in_=mp[:].rearrange("p (ol e half go u) -> p e half go ol u", ol=4, e=2, half=2, go=32, u=2)[
                        :, e, 0
                    ],
                )
        m_codes = const.tile([P, 256], U32, name="m_codes", align_bytes=64)
        m_scales = const.tile([P, 256], U8, name="m_scales", align_bytes=64)
        nc.vector.quantize_mx(out=m_codes[:].bitcast(FP8X4), scales=m_scales[:], in_=gm[:])

        transpose_unit(1)
        quantise_unit(0)

        for i in range(2, LAST_FULL + 1):
            transpose_unit(i)
            if i >= 3:
                finish_unit(i - 3)
            quantise_unit(i - 1)
            vector_copy(i)
            multiply_unit(i - 2)

        transpose_unit(15)
        transpose_unit(16)
        finish_unit(12)
        quantise_unit(14)
        multiply_unit(13)
        multiply_unit(14)
        quantise_unit(15)
        finish_unit(13)
        quantise_unit(16)
        multiply_unit(15)
        multiply_unit(16)
        finish_unit(14)
        finish_unit(15)
        finish_unit(16)
